import numpy as np
import ml_dtypes


def mxq(x, axis, fmt="e4m3"):
    dtype, down = {"e4m3": (ml_dtypes.float8_e4m3fn, 7), "e5m2": (ml_dtypes.float8_e5m2, 14)}[fmt]
    v = np.moveaxis(np.asarray(x, np.float32).astype(ml_dtypes.bfloat16).astype(np.float64), axis, -1)
    blocks = v.reshape(v.shape[:-1] + (-1, 32))
    amax = np.abs(blocks).max(-1, keepdims=True)
    byte = np.maximum(np.where(amax > 0, np.frexp(amax)[1] - 1 + 127, 0) - down, 1)
    scale = np.exp2(byte - 127.0)
    codes = (blocks / scale).astype(np.float32).astype(dtype).astype(np.float64)
    return np.moveaxis((codes * scale).reshape(v.shape), -1, axis)


WIDE = False


def mx_kscale(k):
    if not WIDE:
        return np.ones(k)
    levels = np.array([10, -10, 5, -5, 0])
    a = np.random.permutation(np.resize(levels, k // 512 * 4)).reshape(k // 512, 4)
    idx = np.arange(k)
    return np.exp2(a[idx // 512, idx % 128 // 32])


BF16 = ml_dtypes.bfloat16


def bf(x):
    return np.asarray(x, np.float32).astype(BF16)


def f64(x):
    return np.asarray(x).astype(np.float64)


N, Ci, H, W, Co = 4, 512, 16, 16, 512
TAPS = [(1, 1), (0, 1), (1, 0), (1, 2), (2, 1)]
K = len(TAPS)
PAD = 1


def setup_inputs():
    s = mx_kscale(Ci)
    return {"x": bf(np.random.standard_normal((N, Ci, H, W)) * s[None, :, None, None]),
            "weight": bf(np.random.standard_normal((Co, Ci, K)) / np.sqrt(Ci * K) / s[None, :, None])}


def reference(x, weight):
    xq = mxq(f64(x).reshape(N, Ci, H * W), 1, "e4m3")
    wq = mxq(f64(weight), 1, "e4m3")
    outs = []
    for k, (dy, dx) in enumerate(TAPS):
        y = (wq[:, :, k] @ xq).reshape(N, Co, H, W)
        yp = np.pad(y, ((0, 0), (0, 0), (PAD, PAD), (PAD, PAD)))
        outs.append(yp[:, :, dy:dy + H, dx:dx + W])
    return np.stack(outs, axis=0).sum(axis=0)

@@ -1,0 +1,167 @@
+from contextlib import ExitStack
+
+import concourse.mybir as mybir
+from concourse.masks import make_identity
+
+BF16 = mybir.dt.bfloat16
+F32 = mybir.dt.float32
+I32 = mybir.dt.int32
+U32 = mybir.dt.uint32
+U8 = mybir.dt.uint8
+FP8X4 = mybir.dt.float8_e4m3fn_x4
+
+P = 128
+PACK = 4
+IMAGES, CHANNELS, HEIGHT, WIDTH = 4, 512, 16, 16
+OUT_CHANNELS = 512
+PIXELS = HEIGHT * WIDTH
+TAP_OFFSETS = ((0, 0), (-1, 0), (0, -1), (0, 1), (1, 0))
+TAPS = len(TAP_OFFSETS)
+assert CHANNELS == P * PACK
+
+ROW = WIDTH * IMAGES
+ROWS_PER_PASS = 8
+PASS_COLS = ROWS_PER_PASS * ROW
+ROW_GROUPS = HEIGHT // ROWS_PER_PASS
+OUT_TILES = OUT_CHANNELS // P
+PAIR = 2
+WORDS = CHANNELS // PAIR
+TAPS_PER_BANK = 2
+VECTOR_ROWS = 10
+
+FLOPS = 2 * IMAGES * PIXELS * OUT_CHANNELS * CHANNELS * TAPS
+
+
+def tile_spatialconv_pa_kernel(tc, x, weight, out):
+    nc = tc.nc
+    with ExitStack() as ctx:
+        keep = ctx.enter_context(tc.tile_pool(name="keep", bufs=1))
+        stage = ctx.enter_context(tc.tile_pool(name="stage", bufs=2))
+        flipped = ctx.enter_context(tc.psum_pool(name="flipped", bufs=4))
+        sums = ctx.enter_context(tc.psum_pool(name="sums", bufs=4))
+
+        identity = keep.tile([P, P], F32)
+        x_raw = keep.tile([P, IMAGES, PACK * PIXELS], BF16)
+        x_grouped = keep.tile([P, PIXELS * IMAGES * PACK], BF16, align_bytes=64)
+        x_codes = keep.tile([P, (HEIGHT + 2) * ROW], U32, align_bytes=64)
+        x_scales = keep.tile([P, (HEIGHT + 2) * ROW], U8, align_bytes=64)
+        moved_codes = keep.tile([P, 2, HEIGHT * ROW], U32, align_bytes=64)
+        moved_scales = keep.tile([P, 2, HEIGHT * ROW], U8, align_bytes=64)
+        w_raw = keep.tile([P, OUT_TILES, CHANNELS * TAPS], BF16)
+        w_codes = keep.tile([P, OUT_TILES, TAPS, P], U32, align_bytes=64)
+        w_scales = keep.tile([P, OUT_TILES, TAPS, P], U8, align_bytes=64)
+
+        def load_weights(ot):
+            nc.sync.dma_start(
+                out=w_raw[:, ot, :],
+                in_=weight[ot * P : (ot + 1) * P].rearrange("o c k -> o (c k)"),
+            )
+
+        load_weights(0)
+        for n in range(IMAGES):
+            nc.sync.dma_start(
+                out=x_raw[:, n, :],
+                in_=x[n].rearrange("(p j) h w -> p (j h w)", j=PACK),
+            )
+        for ot in range(1, OUT_TILES):
+            load_weights(ot)
+
+        make_identity(nc, identity[:])
+        nc.vector.memset(x_scales[:].bitcast(I32), 0)
+        nc.vector.memset(x_codes[:, 0:ROW].bitcast(I32), 0)
+        nc.vector.memset(x_codes[:, (HEIGHT + 1) * ROW :].bitcast(I32), 0)
+        nc.vector.memset(moved_codes[:].bitcast(I32), 0)
+        nc.vector.memset(moved_scales[:].bitcast(I32), 0)
+
+        def prepare_weights(ot):
+            by_tap = stage.tile([P, TAPS * CHANNELS], BF16)
+            nc.vector.tensor_copy(
+                out=by_tap[:].rearrange("o (k u p e) -> o k u p e", k=TAPS, u=PAIR, e=PAIR),
+                in_=w_raw[:, ot, :].rearrange("o (p u e k) -> o k u p e", k=TAPS, u=PAIR, e=PAIR),
+            )
+            by_tap_words = by_tap[:].bitcast(F32)
+            w_grouped = stage.tile([P, TAPS, P * PACK], BF16, align_bytes=64)
+            for k0 in range(0, TAPS, TAPS_PER_BANK):
+                taps = min(TAPS_PER_BANK, TAPS - k0)
+                bank = flipped.tile([P, TAPS_PER_BANK * PAIR, P], F32)
+                for s in range(taps * PAIR):
+                    first = (k0 * PAIR + s) * P
+                    nc.tensor.transpose(bank[:, s, :], by_tap_words[:, first : first + P], identity[:])
+                nc.scalar.copy(
+                    out=w_grouped[:, k0 : k0 + taps, :]
+                    .bitcast(F32)
+                    .rearrange("p k (o u) -> p k o u", u=PAIR),
+                    in_=bank[:, 0 : taps * PAIR, :].rearrange("p (k u) o -> p k o u", u=PAIR),
+                )
+                nc.vector.quantize_mx(
+                    out=w_codes[:, ot, k0 : k0 + taps, :].rearrange("p k o -> p (k o)").bitcast(FP8X4),
+                    scales=w_scales[:, ot, k0 : k0 + taps, :].rearrange("p k o -> p (k o)"),
+                    in_=w_grouped[:, k0 : k0 + taps, :].rearrange("p k c -> p (k c)"),
+                )
+
+        def prepare_x():
+            grouped_view = x_grouped[:].rearrange("p (f n j) -> p f n j", n=IMAGES, j=PACK)
+            raw_view = x_raw[:].rearrange("p n (j f) -> p f n j", j=PACK)
+            split = VECTOR_ROWS * WIDTH
+            nc.vector.tensor_copy(out=grouped_view[:, 0:split], in_=raw_view[:, 0:split])
+            nc.scalar.copy(out=grouped_view[:, split:], in_=raw_view[:, split:])
+            nc.vector.quantize_mx(
+                out=x_codes[:, ROW : (HEIGHT + 1) * ROW].bitcast(FP8X4),
+                scales=x_scales[:, ROW : (HEIGHT + 1) * ROW],
+                in_=x_grouped[:],
+            )
+            for source, moved, step in (
+                (x_codes, moved_codes, IMAGES),
+                (x_scales, moved_scales, 1),
+            ):
+                row = WIDTH * step
+                rows = source[:].bitcast(I32).rearrange("p (r c) -> p r c", c=row)[:, 1 : HEIGHT + 1, :]
+                to_right = moved[:, 0, :].bitcast(I32).rearrange("p (r c) -> p r c", c=row)
+                to_left = moved[:, 1, :].bitcast(I32).rearrange("p (r c) -> p r c", c=row)
+                nc.vector.tensor_copy(out=to_right[:, :, step:row], in_=rows[:, :, 0 : row - step])
+                nc.vector.tensor_copy(out=to_left[:, :, 0 : row - step], in_=rows[:, :, step:row])
+
+        def moving_operand(tap, first_row):
+            ey, ex = TAP_OFFSETS[tap]
+            if ex == 0:
+                first = (first_row + ey + 1) * ROW
+                return x_codes[:, first : first + PASS_COLS], x_scales[:, first : first + PASS_COLS]
+            side = 0 if ex < 0 else 1
+            first = first_row * ROW
+            return (
+                moved_codes[:, side, first : first + PASS_COLS],
+                moved_scales[:, side, first : first + PASS_COLS],
+            )
+
+        def multiply(ot):
+            result = stage.tile([P, IMAGES, PIXELS], F32)
+            for g in range(ROW_GROUPS):
+                acc = sums.tile([P, PASS_COLS], F32)
+                for tap in range(TAPS):
+                    codes, scales = moving_operand(tap, g * ROWS_PER_PASS)
+                    nc.tensor.matmul_mx(
+                        out=acc[:],
+                        lhsT=w_codes[:, ot, tap, :].bitcast(FP8X4),
+                        lhsT_scale=w_scales[:, ot, tap, :],
+                        rhs=codes.bitcast(FP8X4),
+                        rhs_scale=scales,
+                        start=(tap == 0),
+                        stop=(tap == TAPS - 1),
+                    )
+                pixels = slice(g * ROWS_PER_PASS * WIDTH, (g + 1) * ROWS_PER_PASS * WIDTH)
+                by_image = acc[:].rearrange("p (f n) -> p n f", n=IMAGES)
+                if g % 2 == 0:
+                    nc.scalar.copy(out=result[:, :, pixels], in_=by_image)
+                else:
+                    nc.vector.tensor_copy(out=result[:, :, pixels], in_=by_image)
+            nc.sync.dma_start(
+                out=out[:, ot * P : (ot + 1) * P].rearrange("n o h w -> o n (h w)"),
+                in_=result[:],
+            )
+
+        prepare_weights(0)
+        prepare_x()
+        for ot in range(OUT_TILES):
+            if ot + 1 < OUT_TILES:
+                prepare_weights(ot + 1)
+            multiply(ot)

@@ -25,9 +25,10 @@ PASS_COLS = ROWS_PER_PASS * ROW
 ROW_GROUPS = HEIGHT // ROWS_PER_PASS
 OUT_TILES = OUT_CHANNELS // P
 PAIR = 2
-WORDS = CHANNELS // PAIR
 TAPS_PER_BANK = 2
-VECTOR_ROWS = 10
+STRAIGHT_TAPS = tuple(k for k in range(TAPS) if TAP_OFFSETS[k][1] == 0)
+SIDE_TAPS = tuple(k for k in range(TAPS) if TAP_OFFSETS[k][1] != 0)
+VECTOR_TAPS = 3
 
 FLOPS = 2 * IMAGES * PIXELS * OUT_CHANNELS * CHANNELS * TAPS
 
@@ -38,7 +39,8 @@ def tile_spatialconv_pa_kernel(tc, x, weight, out):
         keep = ctx.enter_context(tc.tile_pool(name="keep", bufs=1))
         stage = ctx.enter_context(tc.tile_pool(name="stage", bufs=2))
         flipped = ctx.enter_context(tc.psum_pool(name="flipped", bufs=4))
-        sums = ctx.enter_context(tc.psum_pool(name="sums", bufs=4))
+        sums = ctx.enter_context(tc.psum_pool(name="sums", bufs=2))
+        ctx.enter_context(tc.manual_schedule())
 
         identity = keep.tile([P, P], F32)
         x_raw = keep.tile([P, IMAGES, PACK * PIXELS], BF16)
@@ -51,20 +53,16 @@ def tile_spatialconv_pa_kernel(tc, x, weight, out):
         w_codes = keep.tile([P, OUT_TILES, TAPS, P], U32, align_bytes=64)
         w_scales = keep.tile([P, OUT_TILES, TAPS, P], U8, align_bytes=64)
 
-        def load_weights(ot):
-            nc.sync.dma_start(
-                out=w_raw[:, ot, :],
-                in_=weight[ot * P : (ot + 1) * P].rearrange("o c k -> o (c k)"),
-            )
-
-        load_weights(0)
         for n in range(IMAGES):
             nc.sync.dma_start(
                 out=x_raw[:, n, :],
                 in_=x[n].rearrange("(p j) h w -> p (j h w)", j=PACK),
             )
-        for ot in range(1, OUT_TILES):
-            load_weights(ot)
+        for ot in range(OUT_TILES):
+            nc.sync.dma_start(
+                out=w_raw[:, ot, :],
+                in_=weight[ot * P : (ot + 1) * P].rearrange("o c k -> o (c k)"),
+            )
 
         make_identity(nc, identity[:])
         nc.vector.memset(x_scales[:].bitcast(I32), 0)
@@ -73,12 +71,50 @@ def tile_spatialconv_pa_kernel(tc, x, weight, out):
         nc.vector.memset(moved_codes[:].bitcast(I32), 0)
         nc.vector.memset(moved_scales[:].bitcast(I32), 0)
 
-        def prepare_weights(ot):
-            by_tap = stage.tile([P, TAPS * CHANNELS], BF16)
-            nc.vector.tensor_copy(
-                out=by_tap[:].rearrange("o (k u p e) -> o k u p e", k=TAPS, u=PAIR, e=PAIR),
-                in_=w_raw[:, ot, :].rearrange("o (p u e k) -> o k u p e", k=TAPS, u=PAIR, e=PAIR),
+        def regroup_x():
+            grouped_view = x_grouped[:].rearrange("p (f n j) -> p n f j", n=IMAGES, j=PACK)
+            for n in range(IMAGES):
+                nc.vector.tensor_copy(
+                    out=grouped_view[:, n],
+                    in_=x_raw[:, n, :].rearrange("p (j f) -> p f j", j=PACK),
+                )
+
+        def quantise_x():
+            nc.vector.quantize_mx(
+                out=x_codes[:, ROW : (HEIGHT + 1) * ROW].bitcast(FP8X4),
+                scales=x_scales[:, ROW : (HEIGHT + 1) * ROW],
+                in_=x_grouped[:],
             )
+
+        def move_x():
+            for side in range(2):
+                for source, moved, step in (
+                    (x_codes, moved_codes, IMAGES),
+                    (x_scales, moved_scales, 1),
+                ):
+                    row = WIDTH * step
+                    rows = source[:].bitcast(I32).rearrange("p (r c) -> p r c", c=row)
+                    rows = rows[:, 1 : HEIGHT + 1, :]
+                    target = moved[:, side, :].bitcast(I32).rearrange("p (r c) -> p r c", c=row)
+                    if side == 0:
+                        nc.vector.tensor_copy(out=target[:, :, step:row], in_=rows[:, :, 0 : row - step])
+                    else:
+                        nc.vector.tensor_copy(out=target[:, :, 0 : row - step], in_=rows[:, :, step:row])
+
+        def sort_by_tap(ot):
+            by_tap = stage.tile([P, TAPS * CHANNELS], BF16)
+            source = w_raw[:, ot, :].rearrange("o (p u e k) -> o u p e k", u=PAIR, e=PAIR, k=TAPS)
+            target = by_tap[:].rearrange("o (k u p e) -> o u p e k", k=TAPS, u=PAIR, e=PAIR)
+            for u in range(PAIR):
+                nc.vector.tensor_copy(
+                    out=target[:, u, :, :, 0:VECTOR_TAPS], in_=source[:, u, :, :, 0:VECTOR_TAPS]
+                )
+                nc.scalar.copy(
+                    out=target[:, u, :, :, VECTOR_TAPS:], in_=source[:, u, :, :, VECTOR_TAPS:]
+                )
+            return by_tap
+
+        def flip_and_quantise(ot, by_tap):
             by_tap_words = by_tap[:].bitcast(F32)
             w_grouped = stage.tile([P, TAPS, P * PACK], BF16, align_bytes=64)
             for k0 in range(0, TAPS, TAPS_PER_BANK):
@@ -99,28 +135,6 @@ def tile_spatialconv_pa_kernel(tc, x, weight, out):
                     in_=w_grouped[:, k0 : k0 + taps, :].rearrange("p k c -> p (k c)"),
                 )
 
-        def prepare_x():
-            grouped_view = x_grouped[:].rearrange("p (f n j) -> p f n j", n=IMAGES, j=PACK)
-            raw_view = x_raw[:].rearrange("p n (j f) -> p f n j", j=PACK)
-            split = VECTOR_ROWS * WIDTH
-            nc.vector.tensor_copy(out=grouped_view[:, 0:split], in_=raw_view[:, 0:split])
-            nc.scalar.copy(out=grouped_view[:, split:], in_=raw_view[:, split:])
-            nc.vector.quantize_mx(
-                out=x_codes[:, ROW : (HEIGHT + 1) * ROW].bitcast(FP8X4),
-                scales=x_scales[:, ROW : (HEIGHT + 1) * ROW],
-                in_=x_grouped[:],
-            )
-            for source, moved, step in (
-                (x_codes, moved_codes, IMAGES),
-                (x_scales, moved_scales, 1),
-            ):
-                row = WIDTH * step
-                rows = source[:].bitcast(I32).rearrange("p (r c) -> p r c", c=row)[:, 1 : HEIGHT + 1, :]
-                to_right = moved[:, 0, :].bitcast(I32).rearrange("p (r c) -> p r c", c=row)
-                to_left = moved[:, 1, :].bitcast(I32).rearrange("p (r c) -> p r c", c=row)
-                nc.vector.tensor_copy(out=to_right[:, :, step:row], in_=rows[:, :, 0 : row - step])
-                nc.vector.tensor_copy(out=to_left[:, :, 0 : row - step], in_=rows[:, :, step:row])
-
         def moving_operand(tap, first_row):
             ey, ex = TAP_OFFSETS[tap]
             if ex == 0:
@@ -133,35 +147,50 @@ def tile_spatialconv_pa_kernel(tc, x, weight, out):
                 moved_scales[:, side, first : first + PASS_COLS],
             )
 
-        def multiply(ot):
-            result = stage.tile([P, IMAGES, PIXELS], F32)
-            for g in range(ROW_GROUPS):
-                acc = sums.tile([P, PASS_COLS], F32)
-                for tap in range(TAPS):
-                    codes, scales = moving_operand(tap, g * ROWS_PER_PASS)
-                    nc.tensor.matmul_mx(
-                        out=acc[:],
-                        lhsT=w_codes[:, ot, tap, :].bitcast(FP8X4),
-                        lhsT_scale=w_scales[:, ot, tap, :],
-                        rhs=codes.bitcast(FP8X4),
-                        rhs_scale=scales,
-                        start=(tap == 0),
-                        stop=(tap == TAPS - 1),
-                    )
-                pixels = slice(g * ROWS_PER_PASS * WIDTH, (g + 1) * ROWS_PER_PASS * WIDTH)
-                by_image = acc[:].rearrange("p (f n) -> p n f", n=IMAGES)
-                if g % 2 == 0:
-                    nc.scalar.copy(out=result[:, :, pixels], in_=by_image)
-                else:
-                    nc.vector.tensor_copy(out=result[:, :, pixels], in_=by_image)
+        def multiply(ot, g, acc, taps):
+            for tap in taps:
+                codes, scales = moving_operand(tap, g * ROWS_PER_PASS)
+                nc.tensor.matmul_mx(
+                    out=acc[:],
+                    lhsT=w_codes[:, ot, tap, :].bitcast(FP8X4),
+                    lhsT_scale=w_scales[:, ot, tap, :],
+                    rhs=codes.bitcast(FP8X4),
+                    rhs_scale=scales,
+                    start=(tap == STRAIGHT_TAPS[0]),
+                    stop=(tap == SIDE_TAPS[-1]),
+                )
+
+        def store(ot, g, acc):
+            result = stage.tile([P, IMAGES, ROWS_PER_PASS * WIDTH], F32)
+            by_image = acc[:].rearrange("p (f n) -> p n f", n=IMAGES)
+            if g % 2 == 0:
+                nc.scalar.copy(out=result[:], in_=by_image)
+            else:
+                nc.vector.tensor_copy(out=result[:], in_=by_image)
+            rows = slice(g * ROWS_PER_PASS, (g + 1) * ROWS_PER_PASS)
             nc.sync.dma_start(
-                out=out[:, ot * P : (ot + 1) * P].rearrange("n o h w -> o n (h w)"),
+                out=out[:, ot * P : (ot + 1) * P, rows, :].rearrange("n o h w -> o n (h w)"),
                 in_=result[:],
             )
 
-        prepare_weights(0)
-        prepare_x()
+        sorted_weights = {}
+        regroup_x()
+        sorted_weights[0] = sort_by_tap(0)
+        quantise_x()
+        flip_and_quantise(0, sorted_weights[0])
+        sorted_weights[1] = sort_by_tap(1)
+        move_x()
         for ot in range(OUT_TILES):
+            accs = [
+                sums.tile([P, PASS_COLS], F32, name="acc%d" % g, tag="acc%d" % g)
+                for g in range(ROW_GROUPS)
+            ]
+            for g in range(ROW_GROUPS):
+                multiply(ot, g, accs[g], STRAIGHT_TAPS)
+            if ot + 2 < OUT_TILES:
+                sorted_weights[ot + 2] = sort_by_tap(ot + 2)
             if ot + 1 < OUT_TILES:
-                prepare_weights(ot + 1)
-            multiply(ot)
+                flip_and_quantise(ot + 1, sorted_weights[ot + 1])
+            for g in range(ROW_GROUPS):
+                multiply(ot, g, accs[g], SIDE_TAPS)
+                store(ot, g, accs[g])

@@ -163,10 +163,7 @@ def tile_spatialconv_pa_kernel(tc, x, weight, out):
         def store(ot, g, acc):
             result = stage.tile([P, IMAGES, ROWS_PER_PASS * WIDTH], F32)
             by_image = acc[:].rearrange("p (f n) -> p n f", n=IMAGES)
-            if g % 2 == 0:
-                nc.scalar.copy(out=result[:], in_=by_image)
-            else:
-                nc.vector.tensor_copy(out=result[:], in_=by_image)
+            nc.vector.tensor_copy(out=result[:], in_=by_image)
             rows = slice(g * ROWS_PER_PASS, (g + 1) * ROWS_PER_PASS)
             nc.sync.dma_start(
                 out=out[:, ot * P : (ot + 1) * P, rows, :].rearrange("n o h w -> o n (h w)"),

@@ -103,15 +103,11 @@ def tile_spatialconv_pa_kernel(tc, x, weight, out):
 
         def sort_by_tap(ot):
             by_tap = stage.tile([P, TAPS * CHANNELS], BF16)
-            source = w_raw[:, ot, :].rearrange("o (p u e k) -> o u p e k", u=PAIR, e=PAIR, k=TAPS)
-            target = by_tap[:].rearrange("o (k u p e) -> o u p e k", k=TAPS, u=PAIR, e=PAIR)
+            source = w_raw[:, ot, :].rearrange("o (p u e k) -> o u k p e", u=PAIR, e=PAIR, k=TAPS)
+            target = by_tap[:].rearrange("o (k u p e) -> o u k p e", k=TAPS, u=PAIR, e=PAIR)
             for u in range(PAIR):
-                nc.vector.tensor_copy(
-                    out=target[:, u, :, :, 0:VECTOR_TAPS], in_=source[:, u, :, :, 0:VECTOR_TAPS]
-                )
-                nc.scalar.copy(
-                    out=target[:, u, :, :, VECTOR_TAPS:], in_=source[:, u, :, :, VECTOR_TAPS:]
-                )
+                nc.vector.tensor_copy(out=target[:, u, 0:VECTOR_TAPS], in_=source[:, u, 0:VECTOR_TAPS])
+                nc.scalar.copy(out=target[:, u, VECTOR_TAPS:], in_=source[:, u, VECTOR_TAPS:])
             return by_tap
 
         def flip_and_quantise(ot, by_tap):
@@ -163,7 +159,10 @@ def tile_spatialconv_pa_kernel(tc, x, weight, out):
         def store(ot, g, acc):
             result = stage.tile([P, IMAGES, ROWS_PER_PASS * WIDTH], F32)
             by_image = acc[:].rearrange("p (f n) -> p n f", n=IMAGES)
-            nc.vector.tensor_copy(out=result[:], in_=by_image)
+            if g % 2 == 0:
+                nc.scalar.copy(out=result[:], in_=by_image)
+            else:
+                nc.vector.tensor_copy(out=result[:], in_=by_image)
             rows = slice(g * ROWS_PER_PASS, (g + 1) * ROWS_PER_PASS)
             nc.sync.dma_start(
                 out=out[:, ot * P : (ot + 1) * P, rows, :].rearrange("n o h w -> o n (h w)"),

@@ -72,12 +72,10 @@ def tile_spatialconv_pa_kernel(tc, x, weight, out):
         nc.vector.memset(moved_scales[:].bitcast(I32), 0)
 
         def regroup_x():
-            grouped_view = x_grouped[:].rearrange("p (f n j) -> p n f j", n=IMAGES, j=PACK)
-            for n in range(IMAGES):
-                nc.vector.tensor_copy(
-                    out=grouped_view[:, n],
-                    in_=x_raw[:, n, :].rearrange("p (j f) -> p f j", j=PACK),
-                )
+            nc.vector.tensor_copy(
+                out=x_grouped[:].rearrange("p (f n j) -> p f n j", n=IMAGES, j=PACK),
+                in_=x_raw[:].rearrange("p n (j f) -> p f n j", j=PACK),
+            )
 
         def quantise_x():
             nc.vector.quantize_mx(
@@ -103,11 +101,15 @@ def tile_spatialconv_pa_kernel(tc, x, weight, out):
 
         def sort_by_tap(ot):
             by_tap = stage.tile([P, TAPS * CHANNELS], BF16)
-            source = w_raw[:, ot, :].rearrange("o (p u e k) -> o u k p e", u=PAIR, e=PAIR, k=TAPS)
-            target = by_tap[:].rearrange("o (k u p e) -> o u k p e", k=TAPS, u=PAIR, e=PAIR)
+            source = w_raw[:, ot, :].rearrange("o (p u e k) -> o u p e k", u=PAIR, e=PAIR, k=TAPS)
+            target = by_tap[:].rearrange("o (k u p e) -> o u p e k", k=TAPS, u=PAIR, e=PAIR)
             for u in range(PAIR):
-                nc.vector.tensor_copy(out=target[:, u, 0:VECTOR_TAPS], in_=source[:, u, 0:VECTOR_TAPS])
-                nc.scalar.copy(out=target[:, u, VECTOR_TAPS:], in_=source[:, u, VECTOR_TAPS:])
+                nc.vector.tensor_copy(
+                    out=target[:, u, :, :, 0:VECTOR_TAPS], in_=source[:, u, :, :, 0:VECTOR_TAPS]
+                )
+                nc.scalar.copy(
+                    out=target[:, u, :, :, VECTOR_TAPS:], in_=source[:, u, :, :, VECTOR_TAPS:]
+                )
             return by_tap
 
         def flip_and_quantise(ot, by_tap):

@@ -29,6 +29,7 @@ TAPS_PER_BANK = 2
 STRAIGHT_TAPS = tuple(k for k in range(TAPS) if TAP_OFFSETS[k][1] == 0)
 SIDE_TAPS = tuple(k for k in range(TAPS) if TAP_OFFSETS[k][1] != 0)
 VECTOR_TAPS = 3
+VECTOR_ROWS = 11
 
 FLOPS = 2 * IMAGES * PIXELS * OUT_CHANNELS * CHANNELS * TAPS
 
@@ -72,10 +73,12 @@ def tile_spatialconv_pa_kernel(tc, x, weight, out):
         nc.vector.memset(moved_scales[:].bitcast(I32), 0)
 
         def regroup_x():
-            nc.vector.tensor_copy(
-                out=x_grouped[:].rearrange("p (f n j) -> p f n j", n=IMAGES, j=PACK),
-                in_=x_raw[:].rearrange("p n (j f) -> p f n j", j=PACK),
-            )
+            grouped_view = x_grouped[:].rearrange("p (f n j) -> p n f j", n=IMAGES, j=PACK)
+            split = VECTOR_ROWS * WIDTH
+            for n in range(IMAGES):
+                raw_view = x_raw[:, n, :].rearrange("p (j f) -> p f j", j=PACK)
+                nc.vector.tensor_copy(out=grouped_view[:, n, 0:split], in_=raw_view[:, 0:split])
+                nc.scalar.copy(out=grouped_view[:, n, split:], in_=raw_view[:, split:])
 
         def quantise_x():
             nc.vector.quantize_mx(

@@ -28,6 +28,7 @@ PAIR = 2
 TAPS_PER_BANK = 2
 STRAIGHT_TAPS = tuple(k for k in range(TAPS) if TAP_OFFSETS[k][1] == 0)
 SIDE_TAPS = tuple(k for k in range(TAPS) if TAP_OFFSETS[k][1] != 0)
+BANK_ORDER = (0, 4, 2)
 VECTOR_TAPS = 3
 VECTOR_ROWS = 11
 
@@ -54,16 +55,20 @@ def tile_spatialconv_pa_kernel(tc, x, weight, out):
         w_codes = keep.tile([P, OUT_TILES, TAPS, P], U32, align_bytes=64)
         w_scales = keep.tile([P, OUT_TILES, TAPS, P], U8, align_bytes=64)
 
+        def load_weights(ot):
+            nc.sync.dma_start(
+                out=w_raw[:, ot, :],
+                in_=weight[ot * P : (ot + 1) * P].rearrange("o c k -> o (c k)"),
+            )
+
+        load_weights(0)
         for n in range(IMAGES):
             nc.sync.dma_start(
                 out=x_raw[:, n, :],
                 in_=x[n].rearrange("(p j) h w -> p (j h w)", j=PACK),
             )
-        for ot in range(OUT_TILES):
-            nc.sync.dma_start(
-                out=w_raw[:, ot, :],
-                in_=weight[ot * P : (ot + 1) * P].rearrange("o c k -> o (c k)"),
-            )
+        for ot in range(1, OUT_TILES):
+            load_weights(ot)
 
         make_identity(nc, identity[:])
         nc.vector.memset(x_scales[:].bitcast(I32), 0)
@@ -80,11 +85,12 @@ def tile_spatialconv_pa_kernel(tc, x, weight, out):
                 nc.vector.tensor_copy(out=grouped_view[:, n, 0:split], in_=raw_view[:, 0:split])
                 nc.scalar.copy(out=grouped_view[:, n, split:], in_=raw_view[:, split:])
 
-        def quantise_x():
+        def quantise_x(g):
+            first = ROW + g * PASS_COLS
             nc.vector.quantize_mx(
-                out=x_codes[:, ROW : (HEIGHT + 1) * ROW].bitcast(FP8X4),
-                scales=x_scales[:, ROW : (HEIGHT + 1) * ROW],
-                in_=x_grouped[:],
+                out=x_codes[:, first : first + PASS_COLS].bitcast(FP8X4),
+                scales=x_scales[:, first : first + PASS_COLS],
+                in_=x_grouped[:, g * PASS_COLS * PACK : (g + 1) * PASS_COLS * PACK],
             )
 
         def move_x():
@@ -115,10 +121,10 @@ def tile_spatialconv_pa_kernel(tc, x, weight, out):
                 )
             return by_tap
 
-        def flip_and_quantise(ot, by_tap):
+        def flip(ot, by_tap):
             by_tap_words = by_tap[:].bitcast(F32)
             w_grouped = stage.tile([P, TAPS, P * PACK], BF16, align_bytes=64)
-            for k0 in range(0, TAPS, TAPS_PER_BANK):
+            for k0 in BANK_ORDER:
                 taps = min(TAPS_PER_BANK, TAPS - k0)
                 bank = flipped.tile([P, TAPS_PER_BANK * PAIR, P], F32)
                 for s in range(taps * PAIR):
@@ -130,6 +136,11 @@ def tile_spatialconv_pa_kernel(tc, x, weight, out):
                     .rearrange("p k (o u) -> p k o u", u=PAIR),
                     in_=bank[:, 0 : taps * PAIR, :].rearrange("p (k u) o -> p k o u", u=PAIR),
                 )
+            return w_grouped
+
+        def quantise_weights(ot, w_grouped, banks):
+            for k0 in banks:
+                taps = min(TAPS_PER_BANK, TAPS - k0)
                 nc.vector.quantize_mx(
                     out=w_codes[:, ot, k0 : k0 + taps, :].rearrange("p k o -> p (k o)").bitcast(FP8X4),
                     scales=w_scales[:, ot, k0 : k0 + taps, :].rearrange("p k o -> p (k o)"),
@@ -175,10 +186,13 @@ def tile_spatialconv_pa_kernel(tc, x, weight, out):
             )
 
         sorted_weights = {}
-        regroup_x()
         sorted_weights[0] = sort_by_tap(0)
-        quantise_x()
-        flip_and_quantise(0, sorted_weights[0])
+        regroup_x()
+        grouped = flip(0, sorted_weights[0])
+        quantise_x(0)
+        quantise_weights(0, grouped, BANK_ORDER[0:1])
+        quantise_x(1)
+        quantise_weights(0, grouped, BANK_ORDER[1:])
         sorted_weights[1] = sort_by_tap(1)
         move_x()
         for ot in range(OUT_TILES):
@@ -186,12 +200,13 @@ def tile_spatialconv_pa_kernel(tc, x, weight, out):
                 sums.tile([P, PASS_COLS], F32, name="acc%d" % g, tag="acc%d" % g)
                 for g in range(ROW_GROUPS)
             ]
-            for g in range(ROW_GROUPS):
-                multiply(ot, g, accs[g], STRAIGHT_TAPS)
+            for taps in (STRAIGHT_TAPS[0:2], STRAIGHT_TAPS[2:]):
+                for g in range(ROW_GROUPS):
+                    multiply(ot, g, accs[g], taps)
             if ot + 2 < OUT_TILES:
                 sorted_weights[ot + 2] = sort_by_tap(ot + 2)
             if ot + 1 < OUT_TILES:
-                flip_and_quantise(ot + 1, sorted_weights[ot + 1])
+                quantise_weights(ot + 1, flip(ot + 1, sorted_weights[ot + 1]), BANK_ORDER)
             for g in range(ROW_GROUPS):
                 multiply(ot, g, accs[g], SIDE_TAPS)
                 store(ot, g, accs[g])

@@ -29,6 +29,7 @@ TAPS_PER_BANK = 2
 STRAIGHT_TAPS = tuple(k for k in range(TAPS) if TAP_OFFSETS[k][1] == 0)
 SIDE_TAPS = tuple(k for k in range(TAPS) if TAP_OFFSETS[k][1] != 0)
 BANK_ORDER = (0, 4, 2)
+LAST_PIECES = (8, 4, 4)
 VECTOR_TAPS = 3
 VECTOR_ROWS = 11
 
@@ -40,6 +41,7 @@ def tile_spatialconv_pa_kernel(tc, x, weight, out):
     with ExitStack() as ctx:
         keep = ctx.enter_context(tc.tile_pool(name="keep", bufs=1))
         stage = ctx.enter_context(tc.tile_pool(name="stage", bufs=2))
+        results = ctx.enter_context(tc.tile_pool(name="results", bufs=4))
         flipped = ctx.enter_context(tc.psum_pool(name="flipped", bufs=4))
         sums = ctx.enter_context(tc.psum_pool(name="sums", bufs=2))
         ctx.enter_context(tc.manual_schedule())
@@ -147,23 +149,25 @@ def tile_spatialconv_pa_kernel(tc, x, weight, out):
                     in_=w_grouped[:, k0 : k0 + taps, :].rearrange("p k c -> p (k c)"),
                 )
 
-        def moving_operand(tap, first_row):
+        def moving_operand(tap, first_row, rows):
             ey, ex = TAP_OFFSETS[tap]
+            cols = rows * ROW
             if ex == 0:
                 first = (first_row + ey + 1) * ROW
-                return x_codes[:, first : first + PASS_COLS], x_scales[:, first : first + PASS_COLS]
+                return x_codes[:, first : first + cols], x_scales[:, first : first + cols]
             side = 0 if ex < 0 else 1
             first = first_row * ROW
             return (
-                moved_codes[:, side, first : first + PASS_COLS],
-                moved_scales[:, side, first : first + PASS_COLS],
+                moved_codes[:, side, first : first + cols],
+                moved_scales[:, side, first : first + cols],
             )
 
-        def multiply(ot, g, acc, taps):
+        def multiply(ot, piece, acc, taps):
+            first_row, rows = piece
             for tap in taps:
-                codes, scales = moving_operand(tap, g * ROWS_PER_PASS)
+                codes, scales = moving_operand(tap, first_row, rows)
                 nc.tensor.matmul_mx(
-                    out=acc[:],
+                    out=acc[:, 0 : rows * ROW],
                     lhsT=w_codes[:, ot, tap, :].bitcast(FP8X4),
                     lhsT_scale=w_scales[:, ot, tap, :],
                     rhs=codes.bitcast(FP8X4),
@@ -172,16 +176,18 @@ def tile_spatialconv_pa_kernel(tc, x, weight, out):
                     stop=(tap == SIDE_TAPS[-1]),
                 )
 
-        def store(ot, g, acc):
-            result = stage.tile([P, IMAGES, ROWS_PER_PASS * WIDTH], F32)
-            by_image = acc[:].rearrange("p (f n) -> p n f", n=IMAGES)
-            if g % 2 == 0:
+        def store(ot, piece, acc, on_scalar):
+            first_row, rows = piece
+            result = results.tile([P, IMAGES, rows * WIDTH], F32)
+            by_image = acc[:, 0 : rows * ROW].rearrange("p (f n) -> p n f", n=IMAGES)
+            if on_scalar:
                 nc.scalar.copy(out=result[:], in_=by_image)
             else:
                 nc.vector.tensor_copy(out=result[:], in_=by_image)
-            rows = slice(g * ROWS_PER_PASS, (g + 1) * ROWS_PER_PASS)
             nc.sync.dma_start(
-                out=out[:, ot * P : (ot + 1) * P, rows, :].rearrange("n o h w -> o n (h w)"),
+                out=out[:, ot * P : (ot + 1) * P, first_row : first_row + rows, :].rearrange(
+                    "n o h w -> o n (h w)"
+                ),
                 in_=result[:],
             )
 
@@ -195,18 +201,25 @@ def tile_spatialconv_pa_kernel(tc, x, weight, out):
         quantise_weights(0, grouped, BANK_ORDER[1:])
         sorted_weights[1] = sort_by_tap(1)
         move_x()
-        for ot in range(OUT_TILES):
+        halves = tuple((g * ROWS_PER_PASS, ROWS_PER_PASS) for g in range(ROW_GROUPS))
+        for ot in range(OUT_TILES - 1):
             accs = [
                 sums.tile([P, PASS_COLS], F32, name="acc%d" % g, tag="acc%d" % g)
                 for g in range(ROW_GROUPS)
             ]
             for taps in (STRAIGHT_TAPS[0:2], STRAIGHT_TAPS[2:]):
                 for g in range(ROW_GROUPS):
-                    multiply(ot, g, accs[g], taps)
+                    multiply(ot, halves[g], accs[g], taps)
             if ot + 2 < OUT_TILES:
                 sorted_weights[ot + 2] = sort_by_tap(ot + 2)
-            if ot + 1 < OUT_TILES:
-                quantise_weights(ot + 1, flip(ot + 1, sorted_weights[ot + 1]), BANK_ORDER)
+            quantise_weights(ot + 1, flip(ot + 1, sorted_weights[ot + 1]), BANK_ORDER)
             for g in range(ROW_GROUPS):
-                multiply(ot, g, accs[g], SIDE_TAPS)
-                store(ot, g, accs[g])
+                multiply(ot, halves[g], accs[g], SIDE_TAPS)
+                store(ot, halves[g], accs[g], g % 2 == 0)
+        first_row = 0
+        for i, rows in enumerate(LAST_PIECES):
+            acc = sums.tile([P, PASS_COLS], F32, name="acc%d" % (i % 2), tag="acc%d" % (i % 2))
+            piece = (first_row, rows)
+            multiply(OUT_TILES - 1, piece, acc, STRAIGHT_TAPS + SIDE_TAPS)
+            store(OUT_TILES - 1, piece, acc, i % 2 == 0)
+            first_row += rows

@@ -30,6 +30,7 @@ STRAIGHT_TAPS = tuple(k for k in range(TAPS) if TAP_OFFSETS[k][1] == 0)
 SIDE_TAPS = tuple(k for k in range(TAPS) if TAP_OFFSETS[k][1] != 0)
 BANK_ORDER = (0, 4, 2)
 LAST_PIECES = (8, 4, 4)
+FIRST_PARTS = 2
 VECTOR_TAPS = 3
 VECTOR_ROWS = 11
 
@@ -57,20 +58,23 @@ def tile_spatialconv_pa_kernel(tc, x, weight, out):
         w_codes = keep.tile([P, OUT_TILES, TAPS, P], U32, align_bytes=64)
         w_scales = keep.tile([P, OUT_TILES, TAPS, P], U8, align_bytes=64)
 
-        def load_weights(ot):
-            nc.sync.dma_start(
-                out=w_raw[:, ot, :],
-                in_=weight[ot * P : (ot + 1) * P].rearrange("o c k -> o (c k)"),
-            )
+        def load_weights(ot, parts):
+            rows = weight[ot * P : (ot + 1) * P].rearrange("o c k -> o (c k)")
+            cols = CHANNELS * TAPS // parts
+            for part in range(parts):
+                nc.sync.dma_start(
+                    out=w_raw[:, ot, part * cols : (part + 1) * cols],
+                    in_=rows[:, part * cols : (part + 1) * cols],
+                )
 
-        load_weights(0)
+        load_weights(0, FIRST_PARTS)
         for n in range(IMAGES):
             nc.sync.dma_start(
                 out=x_raw[:, n, :],
                 in_=x[n].rearrange("(p j) h w -> p (j h w)", j=PACK),
             )
         for ot in range(1, OUT_TILES):
-            load_weights(ot)
+            load_weights(ot, 1)
 
         make_identity(nc, identity[:])
         nc.vector.memset(x_scales[:].bitcast(I32), 0)
@@ -110,23 +114,24 @@ def tile_spatialconv_pa_kernel(tc, x, weight, out):
                     else:
                         nc.vector.tensor_copy(out=target[:, :, 0 : row - step], in_=rows[:, :, step:row])
 
-        def sort_by_tap(ot):
+        def sort_by_tap(ot, parts):
             by_tap = stage.tile([P, TAPS * CHANNELS], BF16)
             source = w_raw[:, ot, :].rearrange("o (p u e k) -> o u p e k", u=PAIR, e=PAIR, k=TAPS)
             target = by_tap[:].rearrange("o (k u p e) -> o u p e k", k=TAPS, u=PAIR, e=PAIR)
-            for u in range(PAIR):
-                nc.vector.tensor_copy(
-                    out=target[:, u, :, :, 0:VECTOR_TAPS], in_=source[:, u, :, :, 0:VECTOR_TAPS]
-                )
-                nc.scalar.copy(
-                    out=target[:, u, :, :, VECTOR_TAPS:], in_=source[:, u, :, :, VECTOR_TAPS:]
-                )
+            for part in range(parts):
+                ps = slice(part * P // parts, (part + 1) * P // parts)
+                for u in range(PAIR):
+                    nc.vector.tensor_copy(
+                        out=target[:, u, ps, :, 0:VECTOR_TAPS], in_=source[:, u, ps, :, 0:VECTOR_TAPS]
+                    )
+                    nc.scalar.copy(
+                        out=target[:, u, ps, :, VECTOR_TAPS:], in_=source[:, u, ps, :, VECTOR_TAPS:]
+                    )
             return by_tap
 
-        def flip(ot, by_tap):
+        def flip(by_tap, w_grouped, banks):
             by_tap_words = by_tap[:].bitcast(F32)
-            w_grouped = stage.tile([P, TAPS, P * PACK], BF16, align_bytes=64)
-            for k0 in BANK_ORDER:
+            for k0 in banks:
                 taps = min(TAPS_PER_BANK, TAPS - k0)
                 bank = flipped.tile([P, TAPS_PER_BANK * PAIR, P], F32)
                 for s in range(taps * PAIR):
@@ -138,7 +143,6 @@ def tile_spatialconv_pa_kernel(tc, x, weight, out):
                     .rearrange("p k (o u) -> p k o u", u=PAIR),
                     in_=bank[:, 0 : taps * PAIR, :].rearrange("p (k u) o -> p k o u", u=PAIR),
                 )
-            return w_grouped
 
         def quantise_weights(ot, w_grouped, banks):
             for k0 in banks:
@@ -192,14 +196,17 @@ def tile_spatialconv_pa_kernel(tc, x, weight, out):
             )
 
         sorted_weights = {}
-        sorted_weights[0] = sort_by_tap(0)
+        sorted_weights[0] = sort_by_tap(0, FIRST_PARTS)
         regroup_x()
-        grouped = flip(0, sorted_weights[0])
+        w_grouped = stage.tile([P, TAPS, P * PACK], BF16, align_bytes=64)
+        flip(sorted_weights[0], w_grouped, BANK_ORDER[0:2])
         quantise_x(0)
-        quantise_weights(0, grouped, BANK_ORDER[0:1])
+        quantise_weights(0, w_grouped, BANK_ORDER[0:1])
         quantise_x(1)
-        quantise_weights(0, grouped, BANK_ORDER[1:])
-        sorted_weights[1] = sort_by_tap(1)
+        quantise_weights(0, w_grouped, BANK_ORDER[1:2])
+        sorted_weights[1] = sort_by_tap(1, 1)
+        flip(sorted_weights[0], w_grouped, BANK_ORDER[2:])
+        quantise_weights(0, w_grouped, BANK_ORDER[2:])
         move_x()
         halves = tuple((g * ROWS_PER_PASS, ROWS_PER_PASS) for g in range(ROW_GROUPS))
         for ot in range(OUT_TILES - 1):
@@ -207,12 +214,19 @@ def tile_spatialconv_pa_kernel(tc, x, weight, out):
                 sums.tile([P, PASS_COLS], F32, name="acc%d" % g, tag="acc%d" % g)
                 for g in range(ROW_GROUPS)
             ]
-            for taps in (STRAIGHT_TAPS[0:2], STRAIGHT_TAPS[2:]):
+            for g in range(ROW_GROUPS):
+                multiply(ot, halves[g], accs[g], STRAIGHT_TAPS[0:2])
+            if ot == 0:
                 for g in range(ROW_GROUPS):
-                    multiply(ot, halves[g], accs[g], taps)
+                    multiply(ot, halves[g], accs[g], STRAIGHT_TAPS[2:])
             if ot + 2 < OUT_TILES:
-                sorted_weights[ot + 2] = sort_by_tap(ot + 2)
-            quantise_weights(ot + 1, flip(ot + 1, sorted_weights[ot + 1]), BANK_ORDER)
+                sorted_weights[ot + 2] = sort_by_tap(ot + 2, 1)
+            w_grouped = stage.tile([P, TAPS, P * PACK], BF16, align_bytes=64)
+            flip(sorted_weights[ot + 1], w_grouped, BANK_ORDER)
+            quantise_weights(ot + 1, w_grouped, BANK_ORDER)
+            if ot > 0:
+                for g in range(ROW_GROUPS):
+                    multiply(ot, halves[g], accs[g], STRAIGHT_TAPS[2:])
             for g in range(ROW_GROUPS):
                 multiply(ot, halves[g], accs[g], SIDE_TAPS)
                 store(ot, halves[g], accs[g], g % 2 == 0)

@@ -31,6 +31,7 @@ SIDE_TAPS = tuple(k for k in range(TAPS) if TAP_OFFSETS[k][1] != 0)
 BANK_ORDER = (0, 4, 2)
 LAST_PIECES = (8, 4, 4)
 FIRST_PARTS = 2
+FIRST_VECTOR_TAPS = 2
 VECTOR_TAPS = 3
 VECTOR_ROWS = 11
 
@@ -114,7 +115,7 @@ def tile_spatialconv_pa_kernel(tc, x, weight, out):
                     else:
                         nc.vector.tensor_copy(out=target[:, :, 0 : row - step], in_=rows[:, :, step:row])
 
-        def sort_by_tap(ot, parts):
+        def sort_by_tap(ot, parts, vector_taps):
             by_tap = stage.tile([P, TAPS * CHANNELS], BF16)
             source = w_raw[:, ot, :].rearrange("o (p u e k) -> o u p e k", u=PAIR, e=PAIR, k=TAPS)
             target = by_tap[:].rearrange("o (k u p e) -> o u p e k", k=TAPS, u=PAIR, e=PAIR)
@@ -122,10 +123,10 @@ def tile_spatialconv_pa_kernel(tc, x, weight, out):
                 ps = slice(part * P // parts, (part + 1) * P // parts)
                 for u in range(PAIR):
                     nc.vector.tensor_copy(
-                        out=target[:, u, ps, :, 0:VECTOR_TAPS], in_=source[:, u, ps, :, 0:VECTOR_TAPS]
+                        out=target[:, u, ps, :, 0:vector_taps], in_=source[:, u, ps, :, 0:vector_taps]
                     )
                     nc.scalar.copy(
-                        out=target[:, u, ps, :, VECTOR_TAPS:], in_=source[:, u, ps, :, VECTOR_TAPS:]
+                        out=target[:, u, ps, :, vector_taps:], in_=source[:, u, ps, :, vector_taps:]
                     )
             return by_tap
 
@@ -196,7 +197,7 @@ def tile_spatialconv_pa_kernel(tc, x, weight, out):
             )
 
         sorted_weights = {}
-        sorted_weights[0] = sort_by_tap(0, FIRST_PARTS)
+        sorted_weights[0] = sort_by_tap(0, FIRST_PARTS, FIRST_VECTOR_TAPS)
         regroup_x()
         w_grouped = stage.tile([P, TAPS, P * PACK], BF16, align_bytes=64)
         flip(sorted_weights[0], w_grouped, BANK_ORDER[0:2])
@@ -204,7 +205,7 @@ def tile_spatialconv_pa_kernel(tc, x, weight, out):
         quantise_weights(0, w_grouped, BANK_ORDER[0:1])
         quantise_x(1)
         quantise_weights(0, w_grouped, BANK_ORDER[1:2])
-        sorted_weights[1] = sort_by_tap(1, 1)
+        sorted_weights[1] = sort_by_tap(1, 1, VECTOR_TAPS)
         flip(sorted_weights[0], w_grouped, BANK_ORDER[2:])
         quantise_weights(0, w_grouped, BANK_ORDER[2:])
         move_x()
@@ -220,7 +221,7 @@ def tile_spatialconv_pa_kernel(tc, x, weight, out):
                 for g in range(ROW_GROUPS):
                     multiply(ot, halves[g], accs[g], STRAIGHT_TAPS[2:])
             if ot + 2 < OUT_TILES:
-                sorted_weights[ot + 2] = sort_by_tap(ot + 2, 1)
+                sorted_weights[ot + 2] = sort_by_tap(ot + 2, 1, VECTOR_TAPS)
             w_grouped = stage.tile([P, TAPS, P * PACK], BF16, align_bytes=64)
             flip(sorted_weights[ot + 1], w_grouped, BANK_ORDER)
             quantise_weights(ot + 1, w_grouped, BANK_ORDER)

@@ -31,9 +31,16 @@ SIDE_TAPS = tuple(k for k in range(TAPS) if TAP_OFFSETS[k][1] != 0)
 BANK_ORDER = (0, 4, 2)
 LAST_PIECES = (8, 4, 4)
 FIRST_PARTS = 2
-FIRST_VECTOR_TAPS = 2
 VECTOR_TAPS = 3
-VECTOR_ROWS = 11
+VECTOR_PIXELS = 10 * WIDTH
+BANK_FIRST = 12 * WIDTH
+BANK_PIXELS = PIXELS - BANK_FIRST
+WARM_PRODUCTS = 5
+
+
+def taps_in_bank(k0):
+    return min(TAPS_PER_BANK, TAPS - k0)
+
 
 FLOPS = 2 * IMAGES * PIXELS * OUT_CHANNELS * CHANNELS * TAPS
 
@@ -43,12 +50,14 @@ def tile_spatialconv_pa_kernel(tc, x, weight, out):
     with ExitStack() as ctx:
         keep = ctx.enter_context(tc.tile_pool(name="keep", bufs=1))
         stage = ctx.enter_context(tc.tile_pool(name="stage", bufs=2))
-        results = ctx.enter_context(tc.tile_pool(name="results", bufs=4))
+        results = ctx.enter_context(tc.tile_pool(name="results", bufs=9))
         flipped = ctx.enter_context(tc.psum_pool(name="flipped", bufs=4))
         sums = ctx.enter_context(tc.psum_pool(name="sums", bufs=2))
         ctx.enter_context(tc.manual_schedule())
 
         identity = keep.tile([P, P], F32)
+        identity_bf16 = keep.tile([P, P], BF16)
+        zeros = keep.tile([P, PASS_COLS], BF16)
         x_raw = keep.tile([P, IMAGES, PACK * PIXELS], BF16)
         x_grouped = keep.tile([P, PIXELS * IMAGES * PACK], BF16, align_bytes=64)
         x_codes = keep.tile([P, (HEIGHT + 2) * ROW], U32, align_bytes=64)
@@ -77,20 +86,47 @@ def tile_spatialconv_pa_kernel(tc, x, weight, out):
         for ot in range(1, OUT_TILES):
             load_weights(ot, 1)
 
+        nc.vector.memset(zeros[:].bitcast(I32), 0)
         make_identity(nc, identity[:])
+        make_identity(nc, identity_bf16[:])
         nc.vector.memset(x_scales[:].bitcast(I32), 0)
         nc.vector.memset(x_codes[:, 0:ROW].bitcast(I32), 0)
         nc.vector.memset(x_codes[:, (HEIGHT + 1) * ROW :].bitcast(I32), 0)
-        nc.vector.memset(moved_codes[:].bitcast(I32), 0)
-        nc.vector.memset(moved_scales[:].bitcast(I32), 0)
+        for moved, step in ((moved_codes, IMAGES), (moved_scales, 1)):
+            for side, edge in ((0, 0), (1, WIDTH - 1)):
+                rows = moved[:, side, :].bitcast(I32).rearrange("p (r w c) -> p r w c", w=WIDTH, c=step)
+                nc.vector.memset(rows[:, :, edge, :], 0)
 
-        def regroup_x():
+        def new_bank(dtype, columns):
+            return flipped.tile([P, columns], dtype, name="bank", tag="bank")
+
+        def warm_tensor():
+            bank = new_bank(F32, PASS_COLS)
+            for i in range(WARM_PRODUCTS):
+                nc.tensor.matmul(bank[:], lhsT=zeros[:, 0:P], rhs=zeros[:], start=True, stop=True)
+
+        def regroup_image(n, on_scalar):
             grouped_view = x_grouped[:].rearrange("p (f n j) -> p n f j", n=IMAGES, j=PACK)
-            split = VECTOR_ROWS * WIDTH
+            raw_view = x_raw[:, n, :].rearrange("p (j f) -> p f j", j=PACK)
+            if on_scalar:
+                fs = slice(VECTOR_PIXELS, BANK_FIRST)
+                nc.scalar.copy(out=grouped_view[:, n, fs], in_=raw_view[:, fs])
+            else:
+                fs = slice(0, VECTOR_PIXELS)
+                nc.vector.tensor_copy(out=grouped_view[:, n, fs], in_=raw_view[:, fs])
+
+        def regroup_on_tensor():
+            bank = new_bank(BF16, BANK_PIXELS * IMAGES * PACK)
+            bank_view = bank[:].rearrange("p (f n j) -> p n j f", n=IMAGES, j=PACK)
             for n in range(IMAGES):
-                raw_view = x_raw[:, n, :].rearrange("p (j f) -> p f j", j=PACK)
-                nc.vector.tensor_copy(out=grouped_view[:, n, 0:split], in_=raw_view[:, 0:split])
-                nc.scalar.copy(out=grouped_view[:, n, split:], in_=raw_view[:, split:])
+                nc.tensor.matmul(
+                    bank_view[:, n],
+                    lhsT=identity_bf16[:],
+                    rhs=x_raw[:, n, :].rearrange("p (j f) -> p j f", j=PACK)[:, :, BANK_FIRST:],
+                    start=True,
+                    stop=True,
+                )
+            return bank
 
         def quantise_x(g):
             first = ROW + g * PASS_COLS
@@ -115,44 +151,42 @@ def tile_spatialconv_pa_kernel(tc, x, weight, out):
                     else:
                         nc.vector.tensor_copy(out=target[:, :, 0 : row - step], in_=rows[:, :, step:row])
 
-        def sort_by_tap(ot, parts, vector_taps):
-            by_tap = stage.tile([P, TAPS * CHANNELS], BF16)
+        def sort_by_tap(ot, parts, by_tap, on_scalar):
             source = w_raw[:, ot, :].rearrange("o (p u e k) -> o u p e k", u=PAIR, e=PAIR, k=TAPS)
             target = by_tap[:].rearrange("o (k u p e) -> o u p e k", k=TAPS, u=PAIR, e=PAIR)
+            ks = slice(VECTOR_TAPS, TAPS) if on_scalar else slice(0, VECTOR_TAPS)
+            copy = nc.scalar.copy if on_scalar else nc.vector.tensor_copy
             for part in range(parts):
                 ps = slice(part * P // parts, (part + 1) * P // parts)
                 for u in range(PAIR):
-                    nc.vector.tensor_copy(
-                        out=target[:, u, ps, :, 0:vector_taps], in_=source[:, u, ps, :, 0:vector_taps]
-                    )
-                    nc.scalar.copy(
-                        out=target[:, u, ps, :, vector_taps:], in_=source[:, u, ps, :, vector_taps:]
-                    )
-            return by_tap
+                    copy(out=target[:, u, ps, :, ks], in_=source[:, u, ps, :, ks])
 
-        def flip(by_tap, w_grouped, banks):
+        def flip(by_tap, k0):
             by_tap_words = by_tap[:].bitcast(F32)
-            for k0 in banks:
-                taps = min(TAPS_PER_BANK, TAPS - k0)
-                bank = flipped.tile([P, TAPS_PER_BANK * PAIR, P], F32)
-                for s in range(taps * PAIR):
-                    first = (k0 * PAIR + s) * P
-                    nc.tensor.transpose(bank[:, s, :], by_tap_words[:, first : first + P], identity[:])
-                nc.scalar.copy(
-                    out=w_grouped[:, k0 : k0 + taps, :]
-                    .bitcast(F32)
-                    .rearrange("p k (o u) -> p k o u", u=PAIR),
-                    in_=bank[:, 0 : taps * PAIR, :].rearrange("p (k u) o -> p k o u", u=PAIR),
+            bank = new_bank(F32, TAPS_PER_BANK * PAIR * P)
+            for s in range(taps_in_bank(k0) * PAIR):
+                first = (k0 * PAIR + s) * P
+                nc.tensor.transpose(
+                    bank[:, s * P : (s + 1) * P], by_tap_words[:, first : first + P], identity[:]
                 )
+            return bank
 
-        def quantise_weights(ot, w_grouped, banks):
-            for k0 in banks:
-                taps = min(TAPS_PER_BANK, TAPS - k0)
-                nc.vector.quantize_mx(
-                    out=w_codes[:, ot, k0 : k0 + taps, :].rearrange("p k o -> p (k o)").bitcast(FP8X4),
-                    scales=w_scales[:, ot, k0 : k0 + taps, :].rearrange("p k o -> p (k o)"),
-                    in_=w_grouped[:, k0 : k0 + taps, :].rearrange("p k c -> p (k c)"),
-                )
+        def pair_up(bank, w_grouped, k0):
+            taps = taps_in_bank(k0)
+            nc.scalar.copy(
+                out=w_grouped[:, k0 : k0 + taps, :]
+                .bitcast(F32)
+                .rearrange("p k (o u) -> p k o u", u=PAIR),
+                in_=bank[:, 0 : taps * PAIR * P].rearrange("p (k u o) -> p k o u", u=PAIR, o=P),
+            )
+
+        def quantise_weights(ot, w_grouped, k0):
+            taps = taps_in_bank(k0)
+            nc.vector.quantize_mx(
+                out=w_codes[:, ot, k0 : k0 + taps, :].rearrange("p k o -> p (k o)").bitcast(FP8X4),
+                scales=w_scales[:, ot, k0 : k0 + taps, :].rearrange("p k o -> p (k o)"),
+                in_=w_grouped[:, k0 : k0 + taps, :].rearrange("p k c -> p (k c)"),
+            )
 
         def moving_operand(tap, first_row, rows):
             ey, ex = TAP_OFFSETS[tap]
@@ -196,18 +230,36 @@ def tile_spatialconv_pa_kernel(tc, x, weight, out):
                 in_=result[:],
             )
 
-        sorted_weights = {}
-        sorted_weights[0] = sort_by_tap(0, FIRST_PARTS, FIRST_VECTOR_TAPS)
-        regroup_x()
-        w_grouped = stage.tile([P, TAPS, P * PACK], BF16, align_bytes=64)
-        flip(sorted_weights[0], w_grouped, BANK_ORDER[0:2])
+        def new_sorted():
+            return stage.tile([P, TAPS * CHANNELS], BF16, name="by_tap", tag="by_tap")
+
+        def new_grouped():
+            return stage.tile([P, TAPS, P * PACK], BF16, align_bytes=64, name="grouped", tag="grouped")
+
+        first_bank, second_bank, last_bank = BANK_ORDER
+        warm_tensor()
+        by_tap = new_sorted()
+        w_grouped = new_grouped()
+        sort_by_tap(0, FIRST_PARTS, by_tap, False)
+        sort_by_tap(0, FIRST_PARTS, by_tap, True)
+        banks = [flip(by_tap, k0) for k0 in BANK_ORDER]
+        x_bank = regroup_on_tensor()
+        for n in range(IMAGES):
+            regroup_image(n, False)
+            regroup_image(n, True)
+            if n == 1:
+                pair_up(banks[0], w_grouped, first_bank)
+                pair_up(banks[1], w_grouped, second_bank)
+        nc.scalar.copy(out=x_grouped[:, BANK_FIRST * IMAGES * PACK :], in_=x_bank[:])
+        quantise_weights(0, w_grouped, first_bank)
         quantise_x(0)
-        quantise_weights(0, w_grouped, BANK_ORDER[0:1])
         quantise_x(1)
-        quantise_weights(0, w_grouped, BANK_ORDER[1:2])
-        sorted_weights[1] = sort_by_tap(1, 1, VECTOR_TAPS)
-        flip(sorted_weights[0], w_grouped, BANK_ORDER[2:])
-        quantise_weights(0, w_grouped, BANK_ORDER[2:])
+        quantise_weights(0, w_grouped, second_bank)
+        next_by_tap = new_sorted()
+        sort_by_tap(1, 1, next_by_tap, False)
+        sort_by_tap(1, 1, next_by_tap, True)
+        pair_up(banks[2], w_grouped, last_bank)
+        quantise_weights(0, w_grouped, last_bank)
         move_x()
         halves = tuple((g * ROWS_PER_PASS, ROWS_PER_PASS) for g in range(ROW_GROUPS))
         for ot in range(OUT_TILES - 1):
@@ -220,11 +272,19 @@ def tile_spatialconv_pa_kernel(tc, x, weight, out):
             if ot == 0:
                 for g in range(ROW_GROUPS):
                     multiply(ot, halves[g], accs[g], STRAIGHT_TAPS[2:])
+            by_tap = next_by_tap
+            w_grouped = new_grouped()
+            banks = [flip(by_tap, k0) for k0 in BANK_ORDER]
             if ot + 2 < OUT_TILES:
-                sorted_weights[ot + 2] = sort_by_tap(ot + 2, 1, VECTOR_TAPS)
-            w_grouped = stage.tile([P, TAPS, P * PACK], BF16, align_bytes=64)
-            flip(sorted_weights[ot + 1], w_grouped, BANK_ORDER)
-            quantise_weights(ot + 1, w_grouped, BANK_ORDER)
+                next_by_tap = new_sorted()
+                sort_by_tap(ot + 2, 1, next_by_tap, True)
+                if ot > 0:
+                    sort_by_tap(ot + 2, 1, next_by_tap, False)
+            for k0, bank in zip(BANK_ORDER, banks):
+                pair_up(bank, w_grouped, k0)
+                quantise_weights(ot + 1, w_grouped, k0)
+                if ot == 0 and k0 == first_bank:
+                    sort_by_tap(ot + 2, 1, next_by_tap, False)
             if ot > 0:
                 for g in range(ROW_GROUPS):
                     multiply(ot, halves[g], accs[g], STRAIGHT_TAPS[2:])

@@ -31,7 +31,7 @@ SIDE_TAPS = tuple(k for k in range(TAPS) if TAP_OFFSETS[k][1] != 0)
 BANK_ORDER = (0, 4, 2)
 LAST_PIECES = (8, 4, 4)
 FIRST_PARTS = 2
-VECTOR_TAPS = 3
+VECTOR_TAPS = (3, 3, 2, 3)
 VECTOR_PIXELS = 10 * WIDTH
 BANK_FIRST = 12 * WIDTH
 BANK_PIXELS = PIXELS - BANK_FIRST
@@ -154,7 +154,7 @@ def tile_spatialconv_pa_kernel(tc, x, weight, out):
         def sort_by_tap(ot, parts, by_tap, on_scalar):
             source = w_raw[:, ot, :].rearrange("o (p u e k) -> o u p e k", u=PAIR, e=PAIR, k=TAPS)
             target = by_tap[:].rearrange("o (k u p e) -> o u p e k", k=TAPS, u=PAIR, e=PAIR)
-            ks = slice(VECTOR_TAPS, TAPS) if on_scalar else slice(0, VECTOR_TAPS)
+            ks = slice(VECTOR_TAPS[ot], TAPS) if on_scalar else slice(0, VECTOR_TAPS[ot])
             copy = nc.scalar.copy if on_scalar else nc.vector.tensor_copy
             for part in range(parts):
                 ps = slice(part * P // parts, (part + 1) * P // parts)
@@ -256,9 +256,9 @@ def tile_spatialconv_pa_kernel(tc, x, weight, out):
         quantise_x(1)
         quantise_weights(0, w_grouped, second_bank)
         next_by_tap = new_sorted()
+        pair_up(banks[2], w_grouped, last_bank)
         sort_by_tap(1, 1, next_by_tap, False)
         sort_by_tap(1, 1, next_by_tap, True)
-        pair_up(banks[2], w_grouped, last_bank)
         quantise_weights(0, w_grouped, last_bank)
         move_x()
         halves = tuple((g * ROWS_PER_PASS, ROWS_PER_PASS) for g in range(ROW_GROUPS))
@@ -275,22 +275,23 @@ def tile_spatialconv_pa_kernel(tc, x, weight, out):
             by_tap = next_by_tap
             w_grouped = new_grouped()
             banks = [flip(by_tap, k0) for k0 in BANK_ORDER]
-            if ot + 2 < OUT_TILES:
-                next_by_tap = new_sorted()
-                sort_by_tap(ot + 2, 1, next_by_tap, True)
-                if ot > 0:
-                    sort_by_tap(ot + 2, 1, next_by_tap, False)
             for k0, bank in zip(BANK_ORDER, banks):
                 pair_up(bank, w_grouped, k0)
                 quantise_weights(ot + 1, w_grouped, k0)
-                if ot == 0 and k0 == first_bank:
+                if k0 == first_bank and ot + 2 < OUT_TILES:
+                    next_by_tap = new_sorted()
+                    sort_by_tap(ot + 2, 1, next_by_tap, True)
                     sort_by_tap(ot + 2, 1, next_by_tap, False)
             if ot > 0:
                 for g in range(ROW_GROUPS):
                     multiply(ot, halves[g], accs[g], STRAIGHT_TAPS[2:])
-            for g in range(ROW_GROUPS):
-                multiply(ot, halves[g], accs[g], SIDE_TAPS)
-                store(ot, halves[g], accs[g], g % 2 == 0)
+            side_steps = [(g, (tap,)) for tap in SIDE_TAPS for g in range(ROW_GROUPS)]
+            if ot > 0:
+                side_steps = [(g, SIDE_TAPS) for g in range(ROW_GROUPS)]
+            for g, taps in side_steps:
+                multiply(ot, halves[g], accs[g], taps)
+                if taps[-1] == SIDE_TAPS[-1]:
+                    store(ot, halves[g], accs[g], g % 2 == 0)
         first_row = 0
         for i, rows in enumerate(LAST_PIECES):
             acc = sums.tile([P, PASS_COLS], F32, name="acc%d" % (i % 2), tag="acc%d" % (i % 2))

@@ -36,6 +36,7 @@ VECTOR_PIXELS = 10 * WIDTH
 BANK_FIRST = 12 * WIDTH
 BANK_PIXELS = PIXELS - BANK_FIRST
 WARM_PRODUCTS = 5
+KEEP_WARM_PRODUCTS = 3
 
 
 def taps_in_bank(k0):
@@ -100,9 +101,8 @@ def tile_spatialconv_pa_kernel(tc, x, weight, out):
         def new_bank(dtype, columns):
             return flipped.tile([P, columns], dtype, name="bank", tag="bank")
 
-        def warm_tensor():
-            bank = new_bank(F32, PASS_COLS)
-            for i in range(WARM_PRODUCTS):
+        def warm_tensor(bank, products):
+            for i in range(products):
                 nc.tensor.matmul(bank[:], lhsT=zeros[:, 0:P], rhs=zeros[:], start=True, stop=True)
 
         def regroup_image(n, on_scalar):
@@ -237,13 +237,15 @@ def tile_spatialconv_pa_kernel(tc, x, weight, out):
             return stage.tile([P, TAPS, P * PACK], BF16, align_bytes=64, name="grouped", tag="grouped")
 
         first_bank, second_bank, last_bank = BANK_ORDER
-        warm_tensor()
+        idle_acc = sums.tile([P, PASS_COLS], F32, name="acc1", tag="acc1")
+        warm_tensor(idle_acc, WARM_PRODUCTS)
         by_tap = new_sorted()
         w_grouped = new_grouped()
         sort_by_tap(0, FIRST_PARTS, by_tap, False)
         sort_by_tap(0, FIRST_PARTS, by_tap, True)
         banks = [flip(by_tap, k0) for k0 in BANK_ORDER]
         x_bank = regroup_on_tensor()
+        warm_tensor(idle_acc, KEEP_WARM_PRODUCTS)
         for n in range(IMAGES):
             regroup_image(n, False)
             regroup_image(n, True)

@@ -30,9 +30,10 @@ STRAIGHT_TAPS = tuple(k for k in range(TAPS) if TAP_OFFSETS[k][1] == 0)
 SIDE_TAPS = tuple(k for k in range(TAPS) if TAP_OFFSETS[k][1] != 0)
 BANK_ORDER = (0, 4, 2)
 LAST_PIECES = (8, 4, 4)
-FIRST_PARTS = 2
+FIRST_PARTS = 4
 VECTOR_TAPS = (3, 3, 2, 3)
 VECTOR_PIXELS = 10 * WIDTH
+LAST_VECTOR_PIXELS = ROWS_PER_PASS * WIDTH
 BANK_FIRST = 12 * WIDTH
 BANK_PIXELS = PIXELS - BANK_FIRST
 WARM_PRODUCTS = 5
@@ -108,11 +109,12 @@ def tile_spatialconv_pa_kernel(tc, x, weight, out):
         def regroup_image(n, on_scalar):
             grouped_view = x_grouped[:].rearrange("p (f n j) -> p n f j", n=IMAGES, j=PACK)
             raw_view = x_raw[:, n, :].rearrange("p (j f) -> p f j", j=PACK)
+            split = LAST_VECTOR_PIXELS if n == IMAGES - 1 else VECTOR_PIXELS
             if on_scalar:
-                fs = slice(VECTOR_PIXELS, BANK_FIRST)
+                fs = slice(split, BANK_FIRST)
                 nc.scalar.copy(out=grouped_view[:, n, fs], in_=raw_view[:, fs])
             else:
-                fs = slice(0, VECTOR_PIXELS)
+                fs = slice(0, split)
                 nc.vector.tensor_copy(out=grouped_view[:, n, fs], in_=raw_view[:, fs])
 
         def regroup_on_tensor():

from contextlib import ExitStack

import concourse.mybir as mybir
from concourse.masks import make_identity

BF16 = mybir.dt.bfloat16
F32 = mybir.dt.float32
I32 = mybir.dt.int32
U32 = mybir.dt.uint32
U8 = mybir.dt.uint8
FP8X4 = mybir.dt.float8_e4m3fn_x4

P = 128
PACK = 4
IMAGES, CHANNELS, HEIGHT, WIDTH = 4, 512, 16, 16
OUT_CHANNELS = 512
PIXELS = HEIGHT * WIDTH
TAP_OFFSETS = ((0, 0), (-1, 0), (0, -1), (0, 1), (1, 0))
TAPS = len(TAP_OFFSETS)
assert CHANNELS == P * PACK

ROW = WIDTH * IMAGES
ROWS_PER_PASS = 8
PASS_COLS = ROWS_PER_PASS * ROW
ROW_GROUPS = HEIGHT // ROWS_PER_PASS
OUT_TILES = OUT_CHANNELS // P
PAIR = 2
TAPS_PER_BANK = 2
STRAIGHT_TAPS = tuple(k for k in range(TAPS) if TAP_OFFSETS[k][1] == 0)
SIDE_TAPS = tuple(k for k in range(TAPS) if TAP_OFFSETS[k][1] != 0)
BANK_ORDER = (0, 4, 2)
LAST_PIECES = (8, 4, 4)
FIRST_PARTS = 4
VECTOR_TAPS = (3, 3, 2, 3)
VECTOR_PIXELS = 10 * WIDTH
LAST_VECTOR_PIXELS = ROWS_PER_PASS * WIDTH
BANK_FIRST = 12 * WIDTH
BANK_PIXELS = PIXELS - BANK_FIRST
WARM_PRODUCTS = 5
KEEP_WARM_PRODUCTS = 3


def taps_in_bank(k0):
    return min(TAPS_PER_BANK, TAPS - k0)


FLOPS = 2 * IMAGES * PIXELS * OUT_CHANNELS * CHANNELS * TAPS


def tile_spatialconv_pa_kernel(tc, x, weight, out):
    nc = tc.nc
    with ExitStack() as ctx:
        keep = ctx.enter_context(tc.tile_pool(name="keep", bufs=1))
        stage = ctx.enter_context(tc.tile_pool(name="stage", bufs=2))
        results = ctx.enter_context(tc.tile_pool(name="results", bufs=9))
        flipped = ctx.enter_context(tc.psum_pool(name="flipped", bufs=4))
        sums = ctx.enter_context(tc.psum_pool(name="sums", bufs=2))
        ctx.enter_context(tc.manual_schedule())

        identity = keep.tile([P, P], F32)
        identity_bf16 = keep.tile([P, P], BF16)
        zeros = keep.tile([P, PASS_COLS], BF16)
        x_raw = keep.tile([P, IMAGES, PACK * PIXELS], BF16)
        x_grouped = keep.tile([P, PIXELS * IMAGES * PACK], BF16, align_bytes=64)
        x_codes = keep.tile([P, (HEIGHT + 2) * ROW], U32, align_bytes=64)
        x_scales = keep.tile([P, (HEIGHT + 2) * ROW], U8, align_bytes=64)
        moved_codes = keep.tile([P, 2, HEIGHT * ROW], U32, align_bytes=64)
        moved_scales = keep.tile([P, 2, HEIGHT * ROW], U8, align_bytes=64)
        w_raw = keep.tile([P, OUT_TILES, CHANNELS * TAPS], BF16)
        w_codes = keep.tile([P, OUT_TILES, TAPS, P], U32, align_bytes=64)
        w_scales = keep.tile([P, OUT_TILES, TAPS, P], U8, align_bytes=64)

        def load_weights(ot, parts):
            rows = weight[ot * P : (ot + 1) * P].rearrange("o c k -> o (c k)")
            cols = CHANNELS * TAPS // parts
            for part in range(parts):
                nc.sync.dma_start(
                    out=w_raw[:, ot, part * cols : (part + 1) * cols],
                    in_=rows[:, part * cols : (part + 1) * cols],
                )

        load_weights(0, FIRST_PARTS)
        for n in range(IMAGES):
            nc.sync.dma_start(
                out=x_raw[:, n, :],
                in_=x[n].rearrange("(p j) h w -> p (j h w)", j=PACK),
            )
        for ot in range(1, OUT_TILES):
            load_weights(ot, 1)

        nc.vector.memset(zeros[:].bitcast(I32), 0)
        make_identity(nc, identity[:])
        make_identity(nc, identity_bf16[:])
        nc.vector.memset(x_scales[:].bitcast(I32), 0)
        nc.vector.memset(x_codes[:, 0:ROW].bitcast(I32), 0)
        nc.vector.memset(x_codes[:, (HEIGHT + 1) * ROW :].bitcast(I32), 0)
        for moved, step in ((moved_codes, IMAGES), (moved_scales, 1)):
            for side, edge in ((0, 0), (1, WIDTH - 1)):
                rows = moved[:, side, :].bitcast(I32).rearrange("p (r w c) -> p r w c", w=WIDTH, c=step)
                nc.vector.memset(rows[:, :, edge, :], 0)

        def new_bank(dtype, columns):
            return flipped.tile([P, columns], dtype, name="bank", tag="bank")

        def warm_tensor(bank, products):
            for i in range(products):
                nc.tensor.matmul(bank[:], lhsT=zeros[:, 0:P], rhs=zeros[:], start=True, stop=True)

        def regroup_image(n, on_scalar):
            grouped_view = x_grouped[:].rearrange("p (f n j) -> p n f j", n=IMAGES, j=PACK)
            raw_view = x_raw[:, n, :].rearrange("p (j f) -> p f j", j=PACK)
            split = LAST_VECTOR_PIXELS if n == IMAGES - 1 else VECTOR_PIXELS
            if on_scalar:
                fs = slice(split, BANK_FIRST)
                nc.scalar.copy(out=grouped_view[:, n, fs], in_=raw_view[:, fs])
            else:
                fs = slice(0, split)
                nc.vector.tensor_copy(out=grouped_view[:, n, fs], in_=raw_view[:, fs])

        def regroup_on_tensor():
            bank = new_bank(BF16, BANK_PIXELS * IMAGES * PACK)
            bank_view = bank[:].rearrange("p (f n j) -> p n j f", n=IMAGES, j=PACK)
            for n in range(IMAGES):
                nc.tensor.matmul(
                    bank_view[:, n],
                    lhsT=identity_bf16[:],
                    rhs=x_raw[:, n, :].rearrange("p (j f) -> p j f", j=PACK)[:, :, BANK_FIRST:],
                    start=True,
                    stop=True,
                )
            return bank

        def quantise_x(g):
            first = ROW + g * PASS_COLS
            nc.vector.quantize_mx(
                out=x_codes[:, first : first + PASS_COLS].bitcast(FP8X4),
                scales=x_scales[:, first : first + PASS_COLS],
                in_=x_grouped[:, g * PASS_COLS * PACK : (g + 1) * PASS_COLS * PACK],
            )

        def move_x():
            for side in range(2):
                for source, moved, step in (
                    (x_codes, moved_codes, IMAGES),
                    (x_scales, moved_scales, 1),
                ):
                    row = WIDTH * step
                    rows = source[:].bitcast(I32).rearrange("p (r c) -> p r c", c=row)
                    rows = rows[:, 1 : HEIGHT + 1, :]
                    target = moved[:, side, :].bitcast(I32).rearrange("p (r c) -> p r c", c=row)
                    if side == 0:
                        nc.vector.tensor_copy(out=target[:, :, step:row], in_=rows[:, :, 0 : row - step])
                    else:
                        nc.vector.tensor_copy(out=target[:, :, 0 : row - step], in_=rows[:, :, step:row])

        def sort_by_tap(ot, parts, by_tap, on_scalar):
            source = w_raw[:, ot, :].rearrange("o (p u e k) -> o u p e k", u=PAIR, e=PAIR, k=TAPS)
            target = by_tap[:].rearrange("o (k u p e) -> o u p e k", k=TAPS, u=PAIR, e=PAIR)
            ks = slice(VECTOR_TAPS[ot], TAPS) if on_scalar else slice(0, VECTOR_TAPS[ot])
            copy = nc.scalar.copy if on_scalar else nc.vector.tensor_copy
            for part in range(parts):
                ps = slice(part * P // parts, (part + 1) * P // parts)
                for u in range(PAIR):
                    copy(out=target[:, u, ps, :, ks], in_=source[:, u, ps, :, ks])

        def flip(by_tap, k0):
            by_tap_words = by_tap[:].bitcast(F32)
            bank = new_bank(F32, TAPS_PER_BANK * PAIR * P)
            for s in range(taps_in_bank(k0) * PAIR):
                first = (k0 * PAIR + s) * P
                nc.tensor.transpose(
                    bank[:, s * P : (s + 1) * P], by_tap_words[:, first : first + P], identity[:]
                )
            return bank

        def pair_up(bank, w_grouped, k0):
            taps = taps_in_bank(k0)
            nc.scalar.copy(
                out=w_grouped[:, k0 : k0 + taps, :]
                .bitcast(F32)
                .rearrange("p k (o u) -> p k o u", u=PAIR),
                in_=bank[:, 0 : taps * PAIR * P].rearrange("p (k u o) -> p k o u", u=PAIR, o=P),
            )

        def quantise_weights(ot, w_grouped, k0):
            taps = taps_in_bank(k0)
            nc.vector.quantize_mx(
                out=w_codes[:, ot, k0 : k0 + taps, :].rearrange("p k o -> p (k o)").bitcast(FP8X4),
                scales=w_scales[:, ot, k0 : k0 + taps, :].rearrange("p k o -> p (k o)"),
                in_=w_grouped[:, k0 : k0 + taps, :].rearrange("p k c -> p (k c)"),
            )

        def moving_operand(tap, first_row, rows):
            ey, ex = TAP_OFFSETS[tap]
            cols = rows * ROW
            if ex == 0:
                first = (first_row + ey + 1) * ROW
                return x_codes[:, first : first + cols], x_scales[:, first : first + cols]
            side = 0 if ex < 0 else 1
            first = first_row * ROW
            return (
                moved_codes[:, side, first : first + cols],
                moved_scales[:, side, first : first + cols],
            )

        def multiply(ot, piece, acc, taps):
            first_row, rows = piece
            for tap in taps:
                codes, scales = moving_operand(tap, first_row, rows)
                nc.tensor.matmul_mx(
                    out=acc[:, 0 : rows * ROW],
                    lhsT=w_codes[:, ot, tap, :].bitcast(FP8X4),
                    lhsT_scale=w_scales[:, ot, tap, :],
                    rhs=codes.bitcast(FP8X4),
                    rhs_scale=scales,
                    start=(tap == STRAIGHT_TAPS[0]),
                    stop=(tap == SIDE_TAPS[-1]),
                )

        def store(ot, piece, acc, on_scalar):
            first_row, rows = piece
            result = results.tile([P, IMAGES, rows * WIDTH], F32)
            by_image = acc[:, 0 : rows * ROW].rearrange("p (f n) -> p n f", n=IMAGES)
            if on_scalar:
                nc.scalar.copy(out=result[:], in_=by_image)
            else:
                nc.vector.tensor_copy(out=result[:], in_=by_image)
            nc.sync.dma_start(
                out=out[:, ot * P : (ot + 1) * P, first_row : first_row + rows, :].rearrange(
                    "n o h w -> o n (h w)"
                ),
                in_=result[:],
            )

        def new_sorted():
            return stage.tile([P, TAPS * CHANNELS], BF16, name="by_tap", tag="by_tap")

        def new_grouped():
            return stage.tile([P, TAPS, P * PACK], BF16, align_bytes=64, name="grouped", tag="grouped")

        first_bank, second_bank, last_bank = BANK_ORDER
        idle_acc = sums.tile([P, PASS_COLS], F32, name="acc1", tag="acc1")
        warm_tensor(idle_acc, WARM_PRODUCTS)
        by_tap = new_sorted()
        w_grouped = new_grouped()
        sort_by_tap(0, FIRST_PARTS, by_tap, False)
        sort_by_tap(0, FIRST_PARTS, by_tap, True)
        banks = [flip(by_tap, k0) for k0 in BANK_ORDER]
        x_bank = regroup_on_tensor()
        warm_tensor(idle_acc, KEEP_WARM_PRODUCTS)
        for n in range(IMAGES):
            regroup_image(n, False)
            regroup_image(n, True)
            if n == 1:
                pair_up(banks[0], w_grouped, first_bank)
                pair_up(banks[1], w_grouped, second_bank)
        nc.scalar.copy(out=x_grouped[:, BANK_FIRST * IMAGES * PACK :], in_=x_bank[:])
        quantise_weights(0, w_grouped, first_bank)
        quantise_x(0)
        quantise_x(1)
        quantise_weights(0, w_grouped, second_bank)
        next_by_tap = new_sorted()
        pair_up(banks[2], w_grouped, last_bank)
        sort_by_tap(1, 1, next_by_tap, False)
        sort_by_tap(1, 1, next_by_tap, True)
        quantise_weights(0, w_grouped, last_bank)
        move_x()
        halves = tuple((g * ROWS_PER_PASS, ROWS_PER_PASS) for g in range(ROW_GROUPS))
        for ot in range(OUT_TILES - 1):
            accs = [
                sums.tile([P, PASS_COLS], F32, name="acc%d" % g, tag="acc%d" % g)
                for g in range(ROW_GROUPS)
            ]
            for g in range(ROW_GROUPS):
                multiply(ot, halves[g], accs[g], STRAIGHT_TAPS[0:2])
            if ot == 0:
                for g in range(ROW_GROUPS):
                    multiply(ot, halves[g], accs[g], STRAIGHT_TAPS[2:])
            by_tap = next_by_tap
            w_grouped = new_grouped()
            banks = [flip(by_tap, k0) for k0 in BANK_ORDER]
            for k0, bank in zip(BANK_ORDER, banks):
                pair_up(bank, w_grouped, k0)
                quantise_weights(ot + 1, w_grouped, k0)
                if k0 == first_bank and ot + 2 < OUT_TILES:
                    next_by_tap = new_sorted()
                    sort_by_tap(ot + 2, 1, next_by_tap, True)
                    sort_by_tap(ot + 2, 1, next_by_tap, False)
            if ot > 0:
                for g in range(ROW_GROUPS):
                    multiply(ot, halves[g], accs[g], STRAIGHT_TAPS[2:])
            side_steps = [(g, (tap,)) for tap in SIDE_TAPS for g in range(ROW_GROUPS)]
            if ot > 0:
                side_steps = [(g, SIDE_TAPS) for g in range(ROW_GROUPS)]
            for g, taps in side_steps:
                multiply(ot, halves[g], accs[g], taps)
                if taps[-1] == SIDE_TAPS[-1]:
                    store(ot, halves[g], accs[g], g % 2 == 0)
        first_row = 0
        for i, rows in enumerate(LAST_PIECES):
            acc = sums.tile([P, PASS_COLS], F32, name="acc%d" % (i % 2), tag="acc%d" % (i % 2))
            piece = (first_row, rows)
            multiply(OUT_TILES - 1, piece, acc, STRAIGHT_TAPS + SIDE_TAPS)
            store(OUT_TILES - 1, piece, acc, i % 2 == 0)
            first_row += rows
